import numpy as np
import ml_dtypes


def mxq(x, axis, fmt="e4m3"):
    dtype, down = {"e4m3": (ml_dtypes.float8_e4m3fn, 7), "e5m2": (ml_dtypes.float8_e5m2, 14)}[fmt]
    v = np.moveaxis(np.asarray(x, np.float32).astype(ml_dtypes.bfloat16).astype(np.float64), axis, -1)
    blocks = v.reshape(v.shape[:-1] + (-1, 32))
    amax = np.abs(blocks).max(-1, keepdims=True)
    byte = np.maximum(np.where(amax > 0, np.frexp(amax)[1] - 1 + 127, 0) - down, 1)
    scale = np.exp2(byte - 127.0)
    codes = (blocks / scale).astype(np.float32).astype(dtype).astype(np.float64)
    return np.moveaxis((codes * scale).reshape(v.shape), -1, axis)


WIDE = False


def mx_kscale(k):
    if not WIDE:
        return np.ones(k)
    levels = np.array([10, -10, 5, -5, 0])
    if k % 512:
        return np.exp2(np.random.permutation(np.resize(levels, k // 32))).repeat(32)
    a = np.empty((k // 512, 16))
    for p in range(k // 512):
        a[p, :8] = np.random.permutation(np.resize(levels, 8))
        for g in range(8):
            far = levels[np.abs(levels - a[p, g]) >= 10]
            a[p, g + 8] = far[np.random.randint(len(far))]
    return np.exp2(a.ravel()).repeat(32)


BF16 = ml_dtypes.bfloat16


def bf(x):
    return np.asarray(x, np.float32).astype(BF16)


def f64(x):
    return np.asarray(x).astype(np.float64)


E2M1 = np.array([0.0, 0.5, 1.0, 1.5, 2.0, 3.0, 4.0, 6.0, -0.0, -0.5, -1.0, -1.5, -2.0, -3.0, -4.0, -6.0])


def pack_weight(w, fmt):
    k, n = w.shape
    w = f64(bf(w)).reshape(k // 32, 32, n)
    amax = np.abs(w).max(1)
    if fmt == "e4m3":
        byte = np.frexp(amax)[1] - 1 + 127 - 7
    else:
        mant, ex = np.frexp(amax / 6.0)
        byte = np.where(mant > 0.5, ex, ex - 1) + 127
    byte = np.clip(np.where(amax > 0, byte, 1), 1, 254)
    scaled = (w * np.exp2(127.0 - byte)[:, None, :]).reshape(k, n).astype(np.float32)
    by_word = np.ascontiguousarray(scaled.reshape(k // 512, 128, 4, n).transpose(0, 1, 3, 2))
    if fmt == "e4m3":
        words = by_word.astype(ml_dtypes.float8_e4m3fn).view(np.uint8)
    else:
        c = by_word.astype(ml_dtypes.float4_e2m1fn).view(np.uint8) & 0xF
        words = c[..., 0::2] | (c[..., 1::2] << 4)
    return np.ascontiguousarray(words), np.ascontiguousarray(byte.astype(np.uint8).reshape(k // 512, 16, n))


def unpack_weight(words, scales, fmt):
    g, p, n, _ = words.shape
    if fmt == "e4m3":
        vals = np.ascontiguousarray(words).view(ml_dtypes.float8_e4m3fn).astype(np.float64)
    else:
        nib = np.empty((g, p, n, 4), np.uint8)
        nib[..., 0::2] = words & 0xF
        nib[..., 1::2] = words >> 4
        vals = E2M1[nib]
    vals = vals * np.repeat(np.exp2(scales.astype(np.float64) - 127.0), 8, axis=1)[..., None]
    return vals.transpose(0, 1, 3, 2).reshape(g * 512, n)
def pack4(w):
    words, scales = pack_weight(w, "e2m1")
    return words.reshape(words.shape[0], 128, -1), scales


def unpack4(words, scales):
    return unpack_weight(words.reshape(words.shape[0], 128, -1, 2), scales, "e2m1")


B, S, D, H = 1, 1024, 512, 512


def draw0():
    s, t = mx_kscale(D), mx_kscale(H)
    audio_feature = bf(np.random.standard_normal((B, S, D)) * s)
    W_phi_words, W_phi_scales = pack4(np.random.standard_normal((D, H)) / np.sqrt(D) / s[:, None] * t)
    b_phi = bf(np.random.standard_normal(H) * 0.2 * t)
    W_theta_words, W_theta_scales = pack4(np.random.standard_normal((D, H)) / np.sqrt(D) / s[:, None] / t)
    b_theta = bf(np.random.standard_normal(H) * 0.2 / t)
    return {"audio_feature": audio_feature,
            "W_phi_words": W_phi_words,
            "W_phi_scales": W_phi_scales,
            "b_phi": b_phi,
            "W_theta_words": W_theta_words,
            "W_theta_scales": W_theta_scales,
            "b_theta": b_theta}


def core(audio_feature, W_phi_words, W_phi_scales, b_phi, W_theta_words, W_theta_scales, b_theta):
    xq = mxq(f64(audio_feature), 2, "e4m3")
    phi_a = (xq @ unpack4(W_phi_words, W_phi_scales)) + f64(b_phi)
    theta_a = (xq @ unpack4(W_theta_words, W_theta_scales)) + f64(b_theta)
    scores = (mxq(phi_a, 2, "e4m3") @ mxq(theta_a, 2, "e4m3").transpose(0, 2, 1)) / np.sqrt(D)
    scores = np.maximum(scores, 0.0)
    return (scores + scores.transpose(0, 2, 1)) * 0.5


def e4m3fn_bytes(y):
    return np.clip(np.asarray(y, np.float64), -448.0, 448.0).astype(np.float32).astype(ml_dtypes.float8_e4m3fn).view(np.uint8)


def e4m3fn_values(b):
    return np.asarray(b, np.uint8).view(ml_dtypes.float8_e4m3fn).astype(np.float64)


def setup_inputs():
    d = draw0()
    x0 = np.asarray(d['audio_feature']).astype(np.float64)
    s = (np.max(np.abs(x0), axis=(0, 1), keepdims=True) / 448.0).astype(np.float32)
    out = {}
    for k, v in d.items():
        if k == 'audio_feature':
            out['audio_feature_bytes'] = e4m3fn_bytes(x0 / s.astype(np.float64))
            out['audio_feature_scale'] = s
        else:
            out[k] = v
    return out


def reference(audio_feature_bytes, audio_feature_scale, W_phi_words, W_phi_scales, b_phi, W_theta_words, W_theta_scales, b_theta):
    return core(e4m3fn_values(audio_feature_bytes) * audio_feature_scale.astype(np.float64), W_phi_words, W_phi_scales, b_phi, W_theta_words, W_theta_scales, b_theta)

@@ -1,0 +1,332 @@
+from contextlib import ExitStack
+import math
+
+import concourse.mybir as mybir
+from concourse.masks import make_identity
+
+TOKENS, FEATURES, HIDDEN = 1024, 512, 512
+FLOPS = 2 * 2 * TOKENS * FEATURES * HIDDEN + 2 * TOKENS * TOKENS * HIDDEN
+HALF_SCALE = 0.5 / math.sqrt(512.0)
+
+F32 = mybir.dt.float32
+BF16 = mybir.dt.bfloat16
+U8 = mybir.dt.uint8
+U32 = mybir.dt.uint32
+I32 = mybir.dt.int32
+E4M3 = mybir.dt.float8_e4m3fn
+E4M3X4 = mybir.dt.float8_e4m3fn_x4
+E2M1X4 = mybir.dt.float4_e2m1fn_x4
+ALU = mybir.AluOpType
+ACT = mybir.ActivationFunctionType
+
+P = 128
+T = 4
+SIZES = (2, 2, 2, 2)
+STARTS = [sum(SIZES[:c]) for c in range(len(SIZES))]
+N_CH = len(SIZES)
+ORDER = """
+wid:0:1:0 turn:0:1:0 wid:0:0:0 wid:1:0:0 turn:0:0:0 xo:0:0:0 xo:0:1:0 turn:1:0:0
+xo:1:0:0 wid:1:1:0 turn:1:1:0 ps:1:0:0 xo:1:1:0 wid:2:1:0 bT:0:0:0 turn:2:1:0
+wid:2:0:0 turn:2:0:0 xo:2:0:0 pw:1:0:0 qx:0:0:0 pw:0:0:0 wide:1:0:1 wide:1:0:0
+qx:1:0:0 xo:2:1:0 wide:1:1:0 bias:0:0:0 takes:1:0:3 takes:1:0:1 takes:1:0:0 takes:1:1:0
+takes:1:1:1 takes:1:0:2 ps:0:0:0 first:0:0:0 wid:3:0:0 first:0:0:1 wide:1:1:1 takes:1:1:3
+takes:1:1:2 wid:3:1:0 turn:3:1:0 xo:3:1:0 qx:2:0:0 wide:1:2:0 turn:3:0:0 xo:3:0:0
+wide:0:1:1 takes:0:1:2 takev:0:0:0 takes:0:1:3 wide:0:1:0 takes:0:1:1 takes:0:1:0 wide:1:2:1
+takes:1:2:3 takes:1:2:2 takev:0:0:1 weave:1:0:0 takes:1:2:0 takes:1:2:1 weave:1:1:0 first:0:2:1
+qx:3:0:0 wide:1:3:1 wide:1:3:0 takes:1:3:1 takes:1:3:0 first:0:2:0 takes:1:3:2 quant:1:1:0
+quant:0:0:0 second:0:0:1 first:0:3:1 weave:0:1:0 u:0:1:0 quant:1:0:0 takes:1:3:3 quant:0:1:0
+second:1:0:1 second:0:1:1 r:1:1:0 second:0:0:0 r:0:0:0 weave:1:2:0 takev:0:2:0 quant:1:2:0
+second:0:1:2 u:1:2:0 takev:0:2:1 quant:0:2:0 second:0:0:2 u:0:2:0 first:0:3:0 stt:0:1:0
+d:0:1:0 second:0:2:2 r:2:2:0 weave:1:3:0 second:1:1:2 stt:1:2:0 store_d:0:1:0 quant:1:3:0
+d:1:2:0 store_d:1:2:0 mT:0:1:0 e:0:1:0 store_e:1:0:0 second:1:0:2 stt:0:2:0 rT:1:1:0
+mT:1:2:0 e:1:2:0 store_e:2:1:0 d:0:2:0 store_d:0:2:0 second:0:2:3 second:0:0:3 u:0:3:0
+takev:0:3:0 takev:0:3:1 quant:0:3:0 rT:0:0:0 add:0:0:0 store_s:0:0:0 mT:0:2:0 rT:2:2:0
+add:2:2:0 store_s:2:2:0 second:1:0:3 stt:0:3:0 d:0:3:0 e:0:2:0 store_e:2:0:0 add:1:1:0
+store_s:1:1:0 store_d:0:3:0 u:2:3:0 second:1:2:3 second:0:1:3 u:1:3:0 mT:0:3:0 e:0:3:0
+store_e:3:0:0 second:0:3:3 r:3:3:0 stt:2:3:0 d:2:3:0 store_d:2:3:0 second:1:1:3 stt:1:3:0
+d:1:3:0 mT:2:3:0 e:2:3:0 store_e:3:2:0 store_d:1:3:0 rT:3:3:0 add:3:3:0 store_s:3:3:0
+mT:1:3:0 e:1:3:0 store_e:3:1:0
+""".split()
+
+
+def tile_selfattention_pa_w4_kernel(tc, x_bytes, x_scale, wp_words, wp_scales, b_phi, wt_words, wt_scales, b_theta, out):
+    nc = tc.nc
+    with ExitStack() as ctx:
+        keep = ctx.enter_context(tc.tile_pool(name="keep", bufs=1))
+        psum = ctx.enter_context(tc.psum_pool(name="psum", bufs=8))
+        ctx.enter_context(tc.manual_schedule())
+
+        w_raw, s_raw, w_perm, s_perm = [], [], [], []
+        for w in range(2):
+            w_raw.append(keep.tile([P, 2 * HIDDEN], U8, name=f"w_raw{w}", align_bytes=64))
+            s_raw.append(keep.tile([P, HIDDEN], U8, name=f"s_raw{w}", align_bytes=64))
+            w_perm.append(keep.tile([P, 2 * HIDDEN], U8, name=f"w_perm{w}", align_bytes=64))
+            s_perm.append(keep.tile([P, HIDDEN], U8, name=f"s_perm{w}", align_bytes=64))
+        x_in, xw, xg, xq, xs, planes_bf, woven = {}, {}, {}, {}, {}, {}, {}
+        for c, n in enumerate(SIZES):
+            x_in[c] = keep.tile([P, n, FEATURES], U8, name=f"x_in{c}")
+            xw[c] = keep.tile([P, n, FEATURES], BF16, name=f"xw{c}")
+            xg[c] = keep.tile([P, n * P, T], BF16, name=f"xg{c}", align_bytes=64)
+            xq[c] = keep.tile([P, n * P], U32, name=f"xq{c}", align_bytes=64)
+            xs[c] = keep.tile([P, n * P], U8, name=f"xs{c}", align_bytes=64)
+            for w in range(2):
+                planes_bf[w, c] = keep.tile([P, T, n * P], BF16, name=f"planes_bf{w}_{c}")
+                woven[w, c] = keep.tile([P, n * P, T], BF16, name=f"woven{w}_{c}", align_bytes=64)
+        codes, planes = [], []
+        for w in range(2):
+            codes.append(keep.tile([P, TOKENS], U32, name=f"codes{w}", align_bytes=64))
+            planes.append(keep.tile([P, TOKENS], U8, name=f"planes{w}", align_bytes=64))
+        k_scale_row = keep.tile([P, FEATURES], F32, name="k_scale_row")
+        bias_rows = keep.tile([P, P], BF16, name="bias_rows")
+        bias = keep.tile([P, 2 * T], F32, name="bias")
+        ident_bf = keep.tile([P, P], BF16, name="ident_bf")
+        ident = keep.tile([P, P], F32, name="ident")
+
+        def rows_of(c):
+            return slice(STARTS[c] * P, (STARTS[c] + SIZES[c]) * P)
+
+        def load_x(c):
+            nc.sync.dma_start(out=x_in[c][:], in_=x_bytes[0, rows_of(c), :].rearrange("(a p) k -> p a k", p=P))
+
+        def load_words(w, src):
+            nc.sync.dma_start(out=w_raw[w][:].bitcast(I32), in_=src[0].bitcast(I32))
+
+        def load_scales(w, src):
+            for q in range(4):
+                nc.sync.dma_start(out=s_raw[w][32 * q : 32 * q + 4, :].bitcast(I32), in_=src[0, 4 * q : 4 * q + 4, :].bitcast(I32))
+
+        nc.scalar.dma_start(out=k_scale_row[:], in_=x_scale.rearrange("o q k -> (o q k)").partition_broadcast(P))
+        nc.vector.memset(s_raw[1][:].bitcast(I32), 0)
+        nc.vector.memset(s_raw[0][:].bitcast(I32), 0)
+        nc.vector.memset(bias_rows[:], 0.0)
+        load_x(0)
+        load_scales(1, wt_scales)
+        load_x(1)
+        load_words(1, wt_words)
+        load_scales(0, wp_scales)
+        load_words(0, wp_words)
+        for c in range(2, N_CH):
+            load_x(c)
+        make_identity(nc, ident[:])
+        for w, b in enumerate((b_phi, b_theta)):
+            nc.gpsimd.dma_start(
+                out=bias_rows[T * w : T * (w + 1), :].rearrange("t (b i) -> t b i", b=16),
+                in_=b.rearrange("(b t i) -> t b i", b=16, t=T),
+            )
+        nc.vector.tensor_copy(out=ident_bf[:], in_=ident[:])
+
+        bank = {}
+
+        def permute(eng, dst, src):
+            eng.tensor_copy(
+                out=dst[:].bitcast(I32).rearrange("p (t b c) -> p t b c", t=T, b=16),
+                in_=src[:].bitcast(I32).rearrange("p (b t c) -> p t b c", t=T, b=16),
+            )
+
+        def pw(w):
+            permute(nc.vector, w_perm[w], w_raw[w])
+
+        def ps(w):
+            permute(nc.vector, s_perm[w], s_raw[w])
+
+        def bias_turn():
+            bk = psum.tile([P, P], BF16, name="bank")
+            bank["bias"] = bk
+            nc.tensor.transpose(bk[:], bias_rows[:], ident_bf[:])
+
+        def bias_take():
+            nc.vector.tensor_copy(out=bias[:], in_=bank["bias"][:, 0 : 2 * T])
+
+        def wid(c, a):
+            nc.vector.tensor_tensor(out=xw[c][:, a, :], in0=x_in[c][:, a, :].bitcast(E4M3), in1=k_scale_row[:], op=ALU.mult)
+
+        def turn(c, a):
+            bk = psum.tile([P, 2, P], F32, name="bank")
+            words = xw[c][:, a, :].bitcast(F32)
+            for u in range(2):
+                nc.tensor.transpose(bk[:, u, :], words[:, u : FEATURES // 2 : 2], ident[:])
+            bank["turn", c, a] = bk
+
+        def xo(c, a):
+            nc.scalar.copy(
+                out=xg[c][:, a * P : (a + 1) * P, :].rearrange("p r t -> p (r t)").bitcast(F32).rearrange("p (r u) -> p r u", u=2),
+                in_=bank["turn", c, a][:].rearrange("p u r -> p r u"),
+            )
+
+        def qx(c):
+            nc.vector.quantize_mx(out=xq[c][:].bitcast(E4M3X4), scales=xs[c][:], in_=xg[c][:].rearrange("p n t -> p (n t)"))
+
+        def mx_first(dst, w, t, c, cols):
+            nc.tensor.matmul_mx(
+                out=dst,
+                lhsT=w_perm[w][:, 2 * P * t : 2 * P * (t + 1)].bitcast(E2M1X4),
+                lhsT_scale=s_perm[w][:, P * t : P * (t + 1)],
+                rhs=xq[c][:, cols].bitcast(E4M3X4),
+                rhs_scale=xs[c][:, cols],
+                start=True,
+                stop=True,
+            )
+
+        def first_tile(w, c, a):
+            bk = psum.tile([P, T, P], F32, name="bank")
+            bank["first", w, c, a] = bk
+            for t in range(T):
+                mx_first(bk[:, t, :], w, t, c, slice(a * P, (a + 1) * P))
+
+        def first_wide(w, c, h):
+            n = SIZES[c]
+            k = T // n
+            bk = psum.tile([P, k, n * P], F32, name="bank")
+            bank["wide", w, c, h] = bk
+            for e in range(k):
+                mx_first(bk[:, e, :], w, k * h + e, c, slice(0, n * P))
+
+        def take_v(w, c, a):
+            nc.vector.tensor_tensor(
+                out=woven[w, c][:, a * P : (a + 1) * P, :],
+                in0=bank["first", w, c, a][:].rearrange("p t r -> p r t"),
+                in1=bias[:, T * w : T * (w + 1)].unsqueeze(1).to_broadcast([P, P, T]),
+                op=ALU.add,
+            )
+
+        def take_s(w, c, t):
+            k = T // SIZES[c]
+            nc.scalar.activation(
+                out=planes_bf[w, c][:, t, :], in_=bank["wide", w, c, t // k][:, t % k, :], func=ACT.Identity, bias=bias[:, T * w + t : T * w + t + 1], scale=1.0
+            )
+
+        def weave(w, c):
+            if False:
+                nc.gpsimd.tensor_scalar(
+                    out=woven[w, c][:], in0=planes_bf[w, c][:].rearrange("p t n -> p n t"), scalar1=1.0, scalar2=0.0, op0=ALU.mult, op1=ALU.add
+                )
+            else:
+                nc.vector.tensor_copy(out=woven[w, c][:], in_=planes_bf[w, c][:].rearrange("p t n -> p n t"))
+
+        def quant(w, c):
+            nc.vector.quantize_mx(out=codes[w][:, rows_of(c)].bitcast(E4M3X4), scales=planes[w][:, rows_of(c)], in_=woven[w, c][:].rearrange("p n t -> p (n t)"))
+
+        def second(w, a, b):
+            bk = psum.tile([P, SIZES[a], SIZES[b] * P], F32, name="bank")
+            bank["ab"[w], a, b] = bk
+            for i in range(SIZES[a]):
+                rows = slice((STARTS[a] + i) * P, (STARTS[a] + i + 1) * P)
+                nc.tensor.matmul_mx(
+                    out=bk[:, i, :],
+                    lhsT=codes[w][:, rows].bitcast(E4M3X4),
+                    lhsT_scale=planes[w][:, rows],
+                    rhs=codes[1 - w][:, rows_of(b)].bitcast(E4M3X4),
+                    rhs_scale=planes[1 - w][:, rows_of(b)],
+                    start=True,
+                    stop=True,
+                )
+
+        sb = {}
+
+        def new(kind, a, b, shape):
+            t = keep.tile(shape, F32, name=f"{kind}{a}_{b}")
+            sb[kind, a, b] = t
+            return t
+
+        def u(a, b):
+            t = new("u", a, b, [P, SIZES[a], SIZES[b] * P])
+            nc.scalar.activation(out=t[:], in_=bank["a", a, b][:], func=ACT.Relu)
+
+        def r(a, b):
+            t = new("r", a, b, [P, SIZES[a], SIZES[b] * P])
+            nc.scalar.activation(out=t[:], in_=bank["a", a, b][:], func=ACT.Relu, scale=HALF_SCALE)
+
+        def stt(a, b):
+            t = new("o", a, b, [P, SIZES[a], SIZES[b] * P])
+            nc.vector.scalar_tensor_tensor(out=t[:], in0=bank["b", a, b][:], scalar=0.0, in1=sb["u", a, b][:], op0=ALU.max, op1=ALU.add)
+
+        def d(a, b):
+            t = new("d", a, b, [P, SIZES[a], SIZES[b] * P])
+            mode = {(0, 3): 'g', (1, 3): 'g', (2, 3): 'g'}.get((a, b), "s")
+            if mode == "g":
+                nc.gpsimd.tensor_scalar(out=t[:], in0=sb["o", a, b][:], scalar1=HALF_SCALE, scalar2=0.0, op0=ALU.mult, op1=ALU.add)
+            elif mode == "s":
+                nc.scalar.activation(out=t[:], in_=sb["o", a, b][:], func=ACT.Copy, scale=HALF_SCALE)
+            else:
+                nc.vector.tensor_scalar(out=t[:], in0=sb["o", a, b][:], scalar1=HALF_SCALE, scalar2=None, op0=ALU.mult)
+
+        def mirror(kind, name, a, b):
+            bk = psum.tile([P, SIZES[b], SIZES[a], P], F32, name="bank")
+            bank[name, a, b] = bk
+            for j in range(SIZES[b]):
+                for i in range(SIZES[a]):
+                    nc.tensor.transpose(bk[:, j, i, :], sb[kind, a, b][:, i, j * P : (j + 1) * P], ident[:])
+
+        def e(a, b):
+            t = new("e", a, b, [P, SIZES[b], SIZES[a] * P])
+            nc.scalar.activation(out=t[:].rearrange("p j q -> p (j q)"), in_=bank["mT", a, b][:].rearrange("p j i q -> p (j i q)"), func=ACT.Copy, scale=HALF_SCALE)
+
+        def add(a, b):
+            t = new("s", a, b, [P, SIZES[a], SIZES[b] * P])
+            nc.vector.tensor_tensor(
+                out=t[:].rearrange("p i q -> p (i q)"), in0=bank["rT", a, b][:].rearrange("p j i q -> p (j i q)"), in1=sb["r", a, b][:].rearrange("p i q -> p (i q)"), op=ALU.add
+            )
+
+        def store(kind, a, b):
+            nc.sync.dma_start(out=out[0, rows_of(a), rows_of(b)].rearrange("(i p) q -> p i q", p=P), in_=sb[kind, min(a, b), max(a, b)][:])
+
+        for step in ORDER:
+            f = step.split(":")
+            name = f[0]
+            x = int(f[1])
+            y = int(f[2])
+            z = int(f[3])
+            if name == "pw":
+                pw(x)
+            elif name == "ps":
+                ps(x)
+            elif name == "bT":
+                bias_turn()
+            elif name == "bias":
+                bias_take()
+            elif name == "wid":
+                wid(x, y)
+            elif name == "turn":
+                turn(x, y)
+            elif name == "xo":
+                xo(x, y)
+            elif name == "qx":
+                qx(x)
+            elif name == "first":
+                first_tile(x, y, z)
+            elif name == "wide":
+                first_wide(x, y, z)
+            elif name == "takev":
+                take_v(x, y, z)
+            elif name == "takes":
+                take_s(x, y, z)
+            elif name == "weave":
+                weave(x, y)
+            elif name == "quant":
+                quant(x, y)
+            elif name == "second":
+                second(x, y, z)
+            elif name == "u":
+                u(x, y)
+            elif name == "r":
+                r(x, y)
+            elif name == "stt":
+                stt(x, y)
+            elif name == "d":
+                d(x, y)
+            elif name == "mT":
+                mirror("o", "mT", x, y)
+            elif name == "rT":
+                mirror("r", "rT", x, y)
+            elif name == "e":
+                e(x, y)
+            elif name == "add":
+                add(x, y)
+            elif name == "store_s":
+                store("s", x, y)
+            elif name == "store_d":
+                store("d", x, y)
+            elif name == "store_e":
+                store("e", x, y)
+            else:
+                raise ValueError("unknown step")

@@ -21,69 +21,54 @@ ACT = mybir.ActivationFunctionType
 
 P = 128
 T = 4
-SIZES = (2, 2, 2, 2)
-STARTS = [sum(SIZES[:c]) for c in range(len(SIZES))]
-N_CH = len(SIZES)
+N_CH = 4
+A = 2
+W = A * P
 ORDER = """
-wid:0:1:0 turn:0:1:0 wid:0:0:0 wid:1:0:0 turn:0:0:0 xo:0:0:0 xo:0:1:0 turn:1:0:0
-xo:1:0:0 wid:1:1:0 turn:1:1:0 ps:1:0:0 xo:1:1:0 wid:2:1:0 bT:0:0:0 turn:2:1:0
-wid:2:0:0 turn:2:0:0 xo:2:0:0 pw:1:0:0 qx:0:0:0 pw:0:0:0 wide:1:0:1 wide:1:0:0
-qx:1:0:0 xo:2:1:0 wide:1:1:0 bias:0:0:0 takes:1:0:3 takes:1:0:1 takes:1:0:0 takes:1:1:0
-takes:1:1:1 takes:1:0:2 ps:0:0:0 first:0:0:0 wid:3:0:0 first:0:0:1 wide:1:1:1 takes:1:1:3
-takes:1:1:2 wid:3:1:0 turn:3:1:0 xo:3:1:0 qx:2:0:0 wide:1:2:0 turn:3:0:0 xo:3:0:0
-wide:0:1:1 takes:0:1:2 takev:0:0:0 takes:0:1:3 wide:0:1:0 takes:0:1:1 takes:0:1:0 wide:1:2:1
-takes:1:2:3 takes:1:2:2 takev:0:0:1 weave:1:0:0 takes:1:2:0 takes:1:2:1 weave:1:1:0 first:0:2:1
-qx:3:0:0 wide:1:3:1 wide:1:3:0 takes:1:3:1 takes:1:3:0 first:0:2:0 takes:1:3:2 quant:1:1:0
-quant:0:0:0 second:0:0:1 first:0:3:1 weave:0:1:0 u:0:1:0 quant:1:0:0 takes:1:3:3 quant:0:1:0
-second:1:0:1 second:0:1:1 r:1:1:0 second:0:0:0 r:0:0:0 weave:1:2:0 takev:0:2:0 quant:1:2:0
-second:0:1:2 u:1:2:0 takev:0:2:1 quant:0:2:0 second:0:0:2 u:0:2:0 first:0:3:0 stt:0:1:0
-d:0:1:0 second:0:2:2 r:2:2:0 weave:1:3:0 second:1:1:2 stt:1:2:0 store_d:0:1:0 quant:1:3:0
-d:1:2:0 store_d:1:2:0 mT:0:1:0 e:0:1:0 store_e:1:0:0 second:1:0:2 stt:0:2:0 rT:1:1:0
-mT:1:2:0 e:1:2:0 store_e:2:1:0 d:0:2:0 store_d:0:2:0 second:0:2:3 second:0:0:3 u:0:3:0
-takev:0:3:0 takev:0:3:1 quant:0:3:0 rT:0:0:0 add:0:0:0 store_s:0:0:0 mT:0:2:0 rT:2:2:0
-add:2:2:0 store_s:2:2:0 second:1:0:3 stt:0:3:0 d:0:3:0 e:0:2:0 store_e:2:0:0 add:1:1:0
-store_s:1:1:0 store_d:0:3:0 u:2:3:0 second:1:2:3 second:0:1:3 u:1:3:0 mT:0:3:0 e:0:3:0
-store_e:3:0:0 second:0:3:3 r:3:3:0 stt:2:3:0 d:2:3:0 store_d:2:3:0 second:1:1:3 stt:1:3:0
-d:1:3:0 mT:2:3:0 e:2:3:0 store_e:3:2:0 store_d:1:3:0 rT:3:3:0 add:3:3:0 store_s:3:3:0
-mT:1:3:0 e:1:3:0 store_e:3:1:0
-""".split()
+cast:0 turn:0 pw:1 cast:1 turn:1 ps:1 xm:0 xm:1 bT bias
+pw:0 ps:0 qx:0 cast:2 turn:2 wide:1:0 xm:2 qx:1 cast:3 qx:2
+tile:0:0 takev:0:0 takes:1:0 weave:1:0 wide:1:1 takes:1:1 weave:1:1 tile:0:1 takev:0:1 turn:3
+xm:3 quant:0:0 tile:0:2 wide:1:2 takes:1:2 quant:1:1 second:0:0:1 u:0:1 quant:0:1 second:0:1:1
+quant:1:0 second:0:0:0 second:1:0:1 r:0:0 qx:3 tile:0:3 r:1:1 takev:0:2 stt:0:1 weave:1:2
+quant:1:2 quant:0:2 d:0:1 store_d:0:1 takev:0:3 wide:1:3 rT:0:0 add:0:0 store_s:0:0 second:0:1:2
+second:1:1:2 takes:1:3 u:1:2 stt:1:2 second:0:0:2 u:0:2 weave:1:3 mT:0:1 e:0:1 store_e:0:1
+second:1:0:2 second:0:2:2 r:2:2 d:1:2 store_d:1:2 mT:1:2 e:1:2 stt:0:2 quant:1:3 store_e:1:2
+quant:0:3 rT:1:1 add:1:1 store_s:1:1 mT:0:2 e:0:2 d:0:2 store_d:0:2 rT:2:2 add:2:2
+store_s:2:2 second:0:1:3 u:1:3 second:0:2:3 u:2:3 second:1:1:3 stt:1:3 store_e:0:2 d:1:3 second:0:3:3
+r:3:3 second:1:2:3 stt:2:3 second:1:0:3 store_d:1:3 second:0:0:3 u:0:3 stt:0:3 d:0:3 mT:1:3
+e:1:3 store_e:1:3 mT:2:3 e:2:3 store_e:2:3 store_d:0:3 mT:0:3 e:0:3 store_e:0:3 rT:3:3
+add:3:3 store_s:3:3 d:2:3 store_d:2:3
+"""
 
 
 def tile_selfattention_pa_w4_kernel(tc, x_bytes, x_scale, wp_words, wp_scales, b_phi, wt_words, wt_scales, b_theta, out):
     nc = tc.nc
     with ExitStack() as ctx:
         keep = ctx.enter_context(tc.tile_pool(name="keep", bufs=1))
+        per_chunk = ctx.enter_context(tc.tile_pool(name="per_chunk", bufs=N_CH))
+        results = ctx.enter_context(tc.tile_pool(name="results", bufs=10))
         psum = ctx.enter_context(tc.psum_pool(name="psum", bufs=8))
         ctx.enter_context(tc.manual_schedule())
 
-        w_raw, s_raw, w_perm, s_perm = [], [], [], []
+        w_raw, s_raw, w_perm, s_perm, codes, planes = [], [], [], [], [], []
         for w in range(2):
             w_raw.append(keep.tile([P, 2 * HIDDEN], U8, name=f"w_raw{w}", align_bytes=64))
             s_raw.append(keep.tile([P, HIDDEN], U8, name=f"s_raw{w}", align_bytes=64))
             w_perm.append(keep.tile([P, 2 * HIDDEN], U8, name=f"w_perm{w}", align_bytes=64))
             s_perm.append(keep.tile([P, HIDDEN], U8, name=f"s_perm{w}", align_bytes=64))
-        x_in, xw, xg, xq, xs, planes_bf, woven = {}, {}, {}, {}, {}, {}, {}
-        for c, n in enumerate(SIZES):
-            x_in[c] = keep.tile([P, n, FEATURES], U8, name=f"x_in{c}")
-            xw[c] = keep.tile([P, n, FEATURES], BF16, name=f"xw{c}")
-            xg[c] = keep.tile([P, n * P, T], BF16, name=f"xg{c}", align_bytes=64)
-            xq[c] = keep.tile([P, n * P], U32, name=f"xq{c}", align_bytes=64)
-            xs[c] = keep.tile([P, n * P], U8, name=f"xs{c}", align_bytes=64)
-            for w in range(2):
-                planes_bf[w, c] = keep.tile([P, T, n * P], BF16, name=f"planes_bf{w}_{c}")
-                woven[w, c] = keep.tile([P, n * P, T], BF16, name=f"woven{w}_{c}", align_bytes=64)
-        codes, planes = [], []
-        for w in range(2):
             codes.append(keep.tile([P, TOKENS], U32, name=f"codes{w}", align_bytes=64))
             planes.append(keep.tile([P, TOKENS], U8, name=f"planes{w}", align_bytes=64))
-        k_scale_row = keep.tile([P, FEATURES], F32, name="k_scale_row")
+        x_in = []
+        for c in range(N_CH):
+            x_in.append(keep.tile([P, A, FEATURES], U8, name=f"x_in{c}"))
+        k_scale = keep.tile([P, T], F32, name="k_scale")
         bias_rows = keep.tile([P, P], BF16, name="bias_rows")
         bias = keep.tile([P, 2 * T], F32, name="bias")
         ident_bf = keep.tile([P, P], BF16, name="ident_bf")
         ident = keep.tile([P, P], F32, name="ident")
 
         def rows_of(c):
-            return slice(STARTS[c] * P, (STARTS[c] + SIZES[c]) * P)
+            return slice(c * W, (c + 1) * W)
 
         def load_x(c):
             nc.sync.dma_start(out=x_in[c][:], in_=x_bytes[0, rows_of(c), :].rearrange("(a p) k -> p a k", p=P))
@@ -95,7 +80,7 @@ def tile_selfattention_pa_w4_kernel(tc, x_bytes, x_scale, wp_words, wp_scales, b
             for q in range(4):
                 nc.sync.dma_start(out=s_raw[w][32 * q : 32 * q + 4, :].bitcast(I32), in_=src[0, 4 * q : 4 * q + 4, :].bitcast(I32))
 
-        nc.scalar.dma_start(out=k_scale_row[:], in_=x_scale.rearrange("o q k -> (o q k)").partition_broadcast(P))
+        nc.scalar.dma_start(out=k_scale[:], in_=x_scale.rearrange("o q (p t) -> p (o q t)", t=T))
         nc.vector.memset(s_raw[1][:].bitcast(I32), 0)
         nc.vector.memset(s_raw[0][:].bitcast(I32), 0)
         nc.vector.memset(bias_rows[:], 0.0)
@@ -105,29 +90,29 @@ def tile_selfattention_pa_w4_kernel(tc, x_bytes, x_scale, wp_words, wp_scales, b
         load_words(1, wt_words)
         load_scales(0, wp_scales)
         load_words(0, wp_words)
-        for c in range(2, N_CH):
-            load_x(c)
-        make_identity(nc, ident[:])
+        load_x(2)
+        load_x(3)
+        make_identity(nc, ident_bf[:])
         for w, b in enumerate((b_phi, b_theta)):
             nc.gpsimd.dma_start(
                 out=bias_rows[T * w : T * (w + 1), :].rearrange("t (b i) -> t b i", b=16),
                 in_=b.rearrange("(b t i) -> t b i", b=16, t=T),
             )
-        nc.vector.tensor_copy(out=ident_bf[:], in_=ident[:])
+        nc.vector.tensor_copy(out=ident[:], in_=ident_bf[:])
 
-        bank = {}
+        bank, tile_of = {}, {}
 
-        def permute(eng, dst, src):
-            eng.tensor_copy(
+        def permute(dst, src):
+            nc.vector.tensor_copy(
                 out=dst[:].bitcast(I32).rearrange("p (t b c) -> p t b c", t=T, b=16),
                 in_=src[:].bitcast(I32).rearrange("p (b t c) -> p t b c", t=T, b=16),
             )
 
         def pw(w):
-            permute(nc.vector, w_perm[w], w_raw[w])
+            permute(w_perm[w], w_raw[w])
 
         def ps(w):
-            permute(nc.vector, s_perm[w], s_raw[w])
+            permute(s_perm[w], s_raw[w])
 
         def bias_turn():
             bk = psum.tile([P, P], BF16, name="bank")
@@ -137,80 +122,100 @@ def tile_selfattention_pa_w4_kernel(tc, x_bytes, x_scale, wp_words, wp_scales, b
         def bias_take():
             nc.vector.tensor_copy(out=bias[:], in_=bank["bias"][:, 0 : 2 * T])
 
-        def wid(c, a):
-            nc.vector.tensor_tensor(out=xw[c][:, a, :], in0=x_in[c][:, a, :].bitcast(E4M3), in1=k_scale_row[:], op=ALU.mult)
+        def cast(c):
+            xw = per_chunk.tile([P, A, FEATURES], BF16, name="xw")
+            tile_of["xw", c] = xw
+            for a in range(A):
+                if c in (0,):
+                    nc.vector.tensor_copy(out=xw[:, a, :], in_=x_in[c][:, a, :].bitcast(E4M3))
+                else:
+                    nc.scalar.copy(out=xw[:, a, :], in_=x_in[c][:, a, :].bitcast(E4M3))
 
-        def turn(c, a):
-            bk = psum.tile([P, 2, P], F32, name="bank")
-            words = xw[c][:, a, :].bitcast(F32)
-            for u in range(2):
-                nc.tensor.transpose(bk[:, u, :], words[:, u : FEATURES // 2 : 2], ident[:])
-            bank["turn", c, a] = bk
+        def turn(c):
+            for a in range(A):
+                bk = psum.tile([P, T, P], BF16, name="bank")
+                bank["turn", c, a] = bk
+                for t in range(T):
+                    nc.tensor.transpose(bk[:, t, :], tile_of["xw", c][:, a, t:FEATURES:T], ident_bf[:])
 
-        def xo(c, a):
-            nc.scalar.copy(
-                out=xg[c][:, a * P : (a + 1) * P, :].rearrange("p r t -> p (r t)").bitcast(F32).rearrange("p (r u) -> p r u", u=2),
-                in_=bank["turn", c, a][:].rearrange("p u r -> p r u"),
-            )
+        def xm(c):
+            xg = per_chunk.tile([P, W, T], BF16, name="xg", align_bytes=64)
+            tile_of["xg", c] = xg
+            for a in range(A):
+                nc.vector.tensor_tensor(
+                    out=xg[:, a * P : (a + 1) * P, :],
+                    in0=bank["turn", c, a][:].rearrange("p t r -> p r t"),
+                    in1=k_scale[:].unsqueeze(1).to_broadcast([P, P, T]),
+                    op=ALU.mult,
+                )
 
         def qx(c):
-            nc.vector.quantize_mx(out=xq[c][:].bitcast(E4M3X4), scales=xs[c][:], in_=xg[c][:].rearrange("p n t -> p (n t)"))
+            xq = per_chunk.tile([P, W], U32, name="xq", align_bytes=64)
+            xs = per_chunk.tile([P, W], U8, name="xs", align_bytes=64)
+            tile_of["xq", c], tile_of["xs", c] = xq, xs
+            nc.vector.quantize_mx(out=xq[:].bitcast(E4M3X4), scales=xs[:], in_=tile_of["xg", c][:].rearrange("p n t -> p (n t)"))
 
         def mx_first(dst, w, t, c, cols):
             nc.tensor.matmul_mx(
                 out=dst,
                 lhsT=w_perm[w][:, 2 * P * t : 2 * P * (t + 1)].bitcast(E2M1X4),
                 lhsT_scale=s_perm[w][:, P * t : P * (t + 1)],
-                rhs=xq[c][:, cols].bitcast(E4M3X4),
-                rhs_scale=xs[c][:, cols],
+                rhs=tile_of["xq", c][:, cols].bitcast(E4M3X4),
+                rhs_scale=tile_of["xs", c][:, cols],
                 start=True,
                 stop=True,
             )
 
-        def first_tile(w, c, a):
-            bk = psum.tile([P, T, P], F32, name="bank")
-            bank["first", w, c, a] = bk
+        def first_tile(w, c):
+            for a in range(A):
+                bk = psum.tile([P, T, P], F32, name="bank")
+                bank["tile", w, c, a] = bk
+                for t in range(T):
+                    mx_first(bk[:, t, :], w, t, c, slice(a * P, (a + 1) * P))
+
+        def first_wide(w, c):
+            for h in range(2):
+                bk = psum.tile([P, 2, W], F32, name="bank")
+                bank["wide", w, c, h] = bk
+                for e in range(2):
+                    mx_first(bk[:, e, :], w, 2 * h + e, c, slice(0, W))
+
+        def take_v(w, c):
+            g = per_chunk.tile([P, W, T], BF16, name=f"woven{w}", align_bytes=64)
+            tile_of["woven", w, c] = g
+            for a in range(A):
+                nc.vector.tensor_tensor(
+                    out=g[:, a * P : (a + 1) * P, :],
+                    in0=bank["tile", w, c, a][:].rearrange("p t r -> p r t"),
+                    in1=bias[:, T * w : T * (w + 1)].unsqueeze(1).to_broadcast([P, P, T]),
+                    op=ALU.add,
+                )
+
+        def take_s(w, c):
+            g = per_chunk.tile([P, T, W], BF16, name=f"rows{w}")
+            tile_of["rows", w, c] = g
             for t in range(T):
-                mx_first(bk[:, t, :], w, t, c, slice(a * P, (a + 1) * P))
-
-        def first_wide(w, c, h):
-            n = SIZES[c]
-            k = T // n
-            bk = psum.tile([P, k, n * P], F32, name="bank")
-            bank["wide", w, c, h] = bk
-            for e in range(k):
-                mx_first(bk[:, e, :], w, k * h + e, c, slice(0, n * P))
-
-        def take_v(w, c, a):
-            nc.vector.tensor_tensor(
-                out=woven[w, c][:, a * P : (a + 1) * P, :],
-                in0=bank["first", w, c, a][:].rearrange("p t r -> p r t"),
-                in1=bias[:, T * w : T * (w + 1)].unsqueeze(1).to_broadcast([P, P, T]),
-                op=ALU.add,
-            )
-
-        def take_s(w, c, t):
-            k = T // SIZES[c]
-            nc.scalar.activation(
-                out=planes_bf[w, c][:, t, :], in_=bank["wide", w, c, t // k][:, t % k, :], func=ACT.Identity, bias=bias[:, T * w + t : T * w + t + 1], scale=1.0
-            )
+                nc.scalar.activation(
+                    out=g[:, t, :], in_=bank["wide", w, c, t // 2][:, t % 2, :], func=ACT.Identity, bias=bias[:, T * w + t : T * w + t + 1], scale=1.0
+                )
 
         def weave(w, c):
-            if False:
-                nc.gpsimd.tensor_scalar(
-                    out=woven[w, c][:], in0=planes_bf[w, c][:].rearrange("p t n -> p n t"), scalar1=1.0, scalar2=0.0, op0=ALU.mult, op1=ALU.add
-                )
+            g = per_chunk.tile([P, W, T], BF16, name=f"woven{w}", align_bytes=64)
+            tile_of["woven", w, c] = g
+            src = tile_of["rows", w, c][:].rearrange("p t n -> p n t")
+            if "g" == "g":
+                nc.gpsimd.tensor_scalar(out=g[:], in0=src, scalar1=1.0, scalar2=0.0, op0=ALU.mult, op1=ALU.add)
             else:
-                nc.vector.tensor_copy(out=woven[w, c][:], in_=planes_bf[w, c][:].rearrange("p t n -> p n t"))
+                nc.vector.tensor_copy(out=g[:], in_=src)
 
         def quant(w, c):
-            nc.vector.quantize_mx(out=codes[w][:, rows_of(c)].bitcast(E4M3X4), scales=planes[w][:, rows_of(c)], in_=woven[w, c][:].rearrange("p n t -> p (n t)"))
+            nc.vector.quantize_mx(out=codes[w][:, rows_of(c)].bitcast(E4M3X4), scales=planes[w][:, rows_of(c)], in_=tile_of["woven", w, c][:].rearrange("p n t -> p (n t)"))
 
         def second(w, a, b):
-            bk = psum.tile([P, SIZES[a], SIZES[b] * P], F32, name="bank")
+            bk = psum.tile([P, A, W], F32, name="bank")
             bank["ab"[w], a, b] = bk
-            for i in range(SIZES[a]):
-                rows = slice((STARTS[a] + i) * P, (STARTS[a] + i + 1) * P)
+            for i in range(A):
+                rows = slice((A * a + i) * P, (A * a + i + 1) * P)
                 nc.tensor.matmul_mx(
                     out=bk[:, i, :],
                     lhsT=codes[w][:, rows].bitcast(E4M3X4),
@@ -221,112 +226,75 @@ def tile_selfattention_pa_w4_kernel(tc, x_bytes, x_scale, wp_words, wp_scales, b
                     stop=True,
                 )
 
-        sb = {}
-
-        def new(kind, a, b, shape):
-            t = keep.tile(shape, F32, name=f"{kind}{a}_{b}")
-            sb[kind, a, b] = t
-            return t
-
         def u(a, b):
-            t = new("u", a, b, [P, SIZES[a], SIZES[b] * P])
+            t = results.tile([P, A, W], F32, name="u")
+            tile_of["u", a, b] = t
             nc.scalar.activation(out=t[:], in_=bank["a", a, b][:], func=ACT.Relu)
 
         def r(a, b):
-            t = new("r", a, b, [P, SIZES[a], SIZES[b] * P])
+            t = results.tile([P, A, W], F32, name="r")
+            tile_of["r", a, b] = t
             nc.scalar.activation(out=t[:], in_=bank["a", a, b][:], func=ACT.Relu, scale=HALF_SCALE)
 
         def stt(a, b):
-            t = new("o", a, b, [P, SIZES[a], SIZES[b] * P])
-            nc.vector.scalar_tensor_tensor(out=t[:], in0=bank["b", a, b][:], scalar=0.0, in1=sb["u", a, b][:], op0=ALU.max, op1=ALU.add)
+            t = results.tile([P, A, W], F32, name="o")
+            tile_of["o", a, b] = t
+            nc.vector.scalar_tensor_tensor(out=t[:], in0=bank["b", a, b][:], scalar=0.0, in1=tile_of["u", a, b][:], op0=ALU.max, op1=ALU.add)
 
         def d(a, b):
-            t = new("d", a, b, [P, SIZES[a], SIZES[b] * P])
-            mode = {(0, 3): 'g', (1, 3): 'g', (2, 3): 'g'}.get((a, b), "s")
+            t = results.tile([P, A, W], F32, name="d")
+            tile_of["d", a, b] = t
+            mode = {}.get((a, b), "g")
             if mode == "g":
-                nc.gpsimd.tensor_scalar(out=t[:], in0=sb["o", a, b][:], scalar1=HALF_SCALE, scalar2=0.0, op0=ALU.mult, op1=ALU.add)
+                nc.gpsimd.tensor_scalar(out=t[:], in0=tile_of["o", a, b][:], scalar1=HALF_SCALE, scalar2=0.0, op0=ALU.mult, op1=ALU.add)
             elif mode == "s":
-                nc.scalar.activation(out=t[:], in_=sb["o", a, b][:], func=ACT.Copy, scale=HALF_SCALE)
+                nc.scalar.activation(out=t[:], in_=tile_of["o", a, b][:], func=ACT.Copy, scale=HALF_SCALE)
             else:
-                nc.vector.tensor_scalar(out=t[:], in0=sb["o", a, b][:], scalar1=HALF_SCALE, scalar2=None, op0=ALU.mult)
+                nc.vector.tensor_scalar(out=t[:], in0=tile_of["o", a, b][:], scalar1=HALF_SCALE, scalar2=None, op0=ALU.mult)
 
         def mirror(kind, name, a, b):
-            bk = psum.tile([P, SIZES[b], SIZES[a], P], F32, name="bank")
+            bk = psum.tile([P, A, A, P], F32, name="bank")
             bank[name, a, b] = bk
-            for j in range(SIZES[b]):
-                for i in range(SIZES[a]):
-                    nc.tensor.transpose(bk[:, j, i, :], sb[kind, a, b][:, i, j * P : (j + 1) * P], ident[:])
+            for j in range(A):
+                for i in range(A):
+                    nc.tensor.transpose(bk[:, j, i, :], tile_of[kind, a, b][:, i, j * P : (j + 1) * P], ident[:])
+
+        def mT(a, b):
+            mirror("o", "m", a, b)
+
+        def rT(a, b):
+            mirror("r", "rt", a, b)
 
         def e(a, b):
-            t = new("e", a, b, [P, SIZES[b], SIZES[a] * P])
-            nc.scalar.activation(out=t[:].rearrange("p j q -> p (j q)"), in_=bank["mT", a, b][:].rearrange("p j i q -> p (j i q)"), func=ACT.Copy, scale=HALF_SCALE)
+            t = results.tile([P, A, W], F32, name="e")
+            tile_of["e", a, b] = t
+            nc.scalar.activation(out=t[:].rearrange("p j q -> p (j q)"), in_=bank["m", a, b][:].rearrange("p j i q -> p (j i q)"), func=ACT.Copy, scale=HALF_SCALE)
 
         def add(a, b):
-            t = new("s", a, b, [P, SIZES[a], SIZES[b] * P])
+            t = results.tile([P, A, W], F32, name="s")
+            tile_of["s", a, b] = t
             nc.vector.tensor_tensor(
-                out=t[:].rearrange("p i q -> p (i q)"), in0=bank["rT", a, b][:].rearrange("p j i q -> p (j i q)"), in1=sb["r", a, b][:].rearrange("p i q -> p (i q)"), op=ALU.add
+                out=t[:].rearrange("p i q -> p (i q)"), in0=bank["rt", a, b][:].rearrange("p j i q -> p (j i q)"), in1=tile_of["r", a, b][:].rearrange("p i q -> p (i q)"), op=ALU.add
             )
 
-        def store(kind, a, b):
-            nc.sync.dma_start(out=out[0, rows_of(a), rows_of(b)].rearrange("(i p) q -> p i q", p=P), in_=sb[kind, min(a, b), max(a, b)][:])
+        def put(a, b, t):
+            nc.sync.dma_start(out=out[0, rows_of(a), rows_of(b)].rearrange("(i p) q -> p i q", p=P), in_=t[:])
 
-        for step in ORDER:
-            f = step.split(":")
-            name = f[0]
-            x = int(f[1])
-            y = int(f[2])
-            z = int(f[3])
-            if name == "pw":
-                pw(x)
-            elif name == "ps":
-                ps(x)
-            elif name == "bT":
-                bias_turn()
-            elif name == "bias":
-                bias_take()
-            elif name == "wid":
-                wid(x, y)
-            elif name == "turn":
-                turn(x, y)
-            elif name == "xo":
-                xo(x, y)
-            elif name == "qx":
-                qx(x)
-            elif name == "first":
-                first_tile(x, y, z)
-            elif name == "wide":
-                first_wide(x, y, z)
-            elif name == "takev":
-                take_v(x, y, z)
-            elif name == "takes":
-                take_s(x, y, z)
-            elif name == "weave":
-                weave(x, y)
-            elif name == "quant":
-                quant(x, y)
-            elif name == "second":
-                second(x, y, z)
-            elif name == "u":
-                u(x, y)
-            elif name == "r":
-                r(x, y)
-            elif name == "stt":
-                stt(x, y)
-            elif name == "d":
-                d(x, y)
-            elif name == "mT":
-                mirror("o", "mT", x, y)
-            elif name == "rT":
-                mirror("r", "rT", x, y)
-            elif name == "e":
-                e(x, y)
-            elif name == "add":
-                add(x, y)
-            elif name == "store_s":
-                store("s", x, y)
-            elif name == "store_d":
-                store("d", x, y)
-            elif name == "store_e":
-                store("e", x, y)
-            else:
-                raise ValueError("unknown step")
+        def store_s(a, b):
+            put(a, b, tile_of["s", a, b])
+
+        def store_d(a, b):
+            put(a, b, tile_of["d", a, b])
+
+        def store_e(a, b):
+            put(b, a, tile_of["e", a, b])
+
+        stages = {
+            "pw": pw, "ps": ps, "bT": bias_turn, "bias": bias_take, "cast": cast, "turn": turn, "xm": xm, "qx": qx,
+            "tile": first_tile, "wide": first_wide, "takev": take_v, "takes": take_s, "weave": weave, "quant": quant,
+            "second": second, "u": u, "r": r, "stt": stt, "d": d, "mT": mT, "rT": rT, "e": e, "add": add,
+            "store_s": store_s, "store_d": store_d, "store_e": store_e,
+        }
+        for step in ORDER.split():
+            parts = step.split(":")
+            stages[parts[0]](*[int(v) for v in parts[1:]])

@@ -21,23 +21,28 @@ ACT = mybir.ActivationFunctionType
 
 P = 128
 T = 4
-N_CH = 4
-A = 2
-W = A * P
+SIZES = (2, 2, 2, 1, 1)
+STARTS = [sum(SIZES[:c]) for c in range(len(SIZES))]
+N_CH = len(SIZES)
 ORDER = """
-cast:0 turn:0 pw:1 cast:1 turn:1 ps:1 xm:0 xm:1 bT bias
-pw:0 ps:0 qx:0 cast:2 turn:2 wide:1:0 xm:2 qx:1 cast:3 qx:2
-tile:0:0 takev:0:0 takes:1:0 weave:1:0 wide:1:1 takes:1:1 weave:1:1 tile:0:1 takev:0:1 turn:3
-xm:3 quant:0:0 tile:0:2 wide:1:2 takes:1:2 quant:1:1 second:0:0:1 u:0:1 quant:0:1 second:0:1:1
-quant:1:0 second:0:0:0 second:1:0:1 r:0:0 qx:3 tile:0:3 r:1:1 takev:0:2 stt:0:1 weave:1:2
-quant:1:2 quant:0:2 d:0:1 store_d:0:1 takev:0:3 wide:1:3 rT:0:0 add:0:0 store_s:0:0 second:0:1:2
-second:1:1:2 takes:1:3 u:1:2 stt:1:2 second:0:0:2 u:0:2 weave:1:3 mT:0:1 e:0:1 store_e:0:1
-second:1:0:2 second:0:2:2 r:2:2 d:1:2 store_d:1:2 mT:1:2 e:1:2 stt:0:2 quant:1:3 store_e:1:2
-quant:0:3 rT:1:1 add:1:1 store_s:1:1 mT:0:2 e:0:2 d:0:2 store_d:0:2 rT:2:2 add:2:2
-store_s:2:2 second:0:1:3 u:1:3 second:0:2:3 u:2:3 second:1:1:3 stt:1:3 store_e:0:2 d:1:3 second:0:3:3
-r:3:3 second:1:2:3 stt:2:3 second:1:0:3 store_d:1:3 second:0:0:3 u:0:3 stt:0:3 d:0:3 mT:1:3
-e:1:3 store_e:1:3 mT:2:3 e:2:3 store_e:2:3 store_d:0:3 mT:0:3 e:0:3 store_e:0:3 rT:3:3
-add:3:3 store_s:3:3 d:2:3 store_d:2:3
+cast:1 cast:0 turn:0 xm:0 ps:1 pw:1 qx:0 cast:3 cast:2 turn:1
+xm:1 bT bias pw:0 wide:1:0 takes:1:0 ps:0 turn:2 qx:1 tile:0:1
+xm:2 takev:0:1 wide:1:1 takes:1:1 cast:4 tile:0:0 turn:3 weave:1:0 qx:2 wide:1:2
+takes:1:2 takev:0:0 tile:0:2 turn:4 xm:3 weave:1:1 quant:0:0 quant:1:1 second:0:0:1 u:0:1
+quant:1:0 second:0:0:0 r:0:0 quant:0:1 second:1:0:1 qx:3 wide:1:3 takes:1:3 second:0:1:1 r:1:1
+tile:0:3 takev:0:2 rT:0:0 weave:1:2 stt:0:1 mT:0:1 e:0:1 quant:1:2 second:0:0:2 second:0:1:2
+u:1:2 quant:0:2 second:1:1:2 second:0:2:2 r:2:2 xm:4 d:0:1 weave:1:3 store_d:0:1 store_e:0:1
+u:0:2 rT:1:1 takev:0:3 second:1:0:2 add:0:0 qx:4 wide:1:4 store_s:0:0 quant:0:3 second:1:0:3
+quant:1:3 second:0:0:3 takes:1:4 stt:1:2 d:1:2 add:1:1 store_s:1:1 second:0:1:3 u:1:3 rT:2:2
+store_d:1:2 u:0:3 stt:0:2 add:2:2 store_s:2:2 mT:1:2 second:1:1:3 stt:1:3 e:1:2 store_e:1:2
+stt:0:3 mT:0:2 e:0:2 weave:1:4 quant:1:4 tile:0:4 takev:0:4 store_e:0:2 second:0:3:3 r:3:3
+mT:1:3 e:1:3 store_e:1:3 d:1:3 store_d:1:3 second:0:2:3 u:2:3 second:0:3:4 d:0:3 store_d:0:3
+second:0:1:4 quant:0:4 second:0:0:4 u:3:4 second:1:2:3 stt:2:3 u:0:4 d:0:2 store_d:0:2 d:2:3
+second:0:2:4 u:2:4 store_d:2:3 mT:0:3 e:0:3 store_e:0:3 second:1:3:4 stt:3:4 u:1:4 second:1:2:4
+stt:2:4 second:0:4:4 r:4:4 second:1:0:4 d:3:4 store_d:3:4 mT:2:3 e:2:3 store_e:2:3 second:1:1:4
+stt:0:4 d:2:4 store_d:2:4 mT:3:4 e:3:4 store_e:3:4 stt:1:4 rT:4:4 add:4:4 store_s:4:4
+rT:3:3 d:0:4 add:3:3 store_s:3:3 store_d:0:4 d:1:4 store_d:1:4 mT:1:4 e:1:4 store_e:1:4
+mT:0:4 e:0:4 store_e:0:4 mT:2:4 e:2:4 store_e:2:4
 """
 
 
@@ -45,8 +50,6 @@ def tile_selfattention_pa_w4_kernel(tc, x_bytes, x_scale, wp_words, wp_scales, b
     nc = tc.nc
     with ExitStack() as ctx:
         keep = ctx.enter_context(tc.tile_pool(name="keep", bufs=1))
-        per_chunk = ctx.enter_context(tc.tile_pool(name="per_chunk", bufs=N_CH))
-        results = ctx.enter_context(tc.tile_pool(name="results", bufs=10))
         psum = ctx.enter_context(tc.psum_pool(name="psum", bufs=8))
         ctx.enter_context(tc.manual_schedule())
 
@@ -58,9 +61,8 @@ def tile_selfattention_pa_w4_kernel(tc, x_bytes, x_scale, wp_words, wp_scales, b
             s_perm.append(keep.tile([P, HIDDEN], U8, name=f"s_perm{w}", align_bytes=64))
             codes.append(keep.tile([P, TOKENS], U32, name=f"codes{w}", align_bytes=64))
             planes.append(keep.tile([P, TOKENS], U8, name=f"planes{w}", align_bytes=64))
-        x_in = []
-        for c in range(N_CH):
-            x_in.append(keep.tile([P, A, FEATURES], U8, name=f"x_in{c}"))
+        x_first = keep.tile([P, SIZES[0], FEATURES], U8, name="x_first")
+        x_rest = keep.tile([P, TOKENS // P - SIZES[0], FEATURES], U8, name="x_rest")
         k_scale = keep.tile([P, T], F32, name="k_scale")
         bias_rows = keep.tile([P, P], BF16, name="bias_rows")
         bias = keep.tile([P, 2 * T], F32, name="bias")
@@ -68,10 +70,14 @@ def tile_selfattention_pa_w4_kernel(tc, x_bytes, x_scale, wp_words, wp_scales, b
         ident = keep.tile([P, P], F32, name="ident")
 
         def rows_of(c):
-            return slice(c * W, (c + 1) * W)
+            return slice(STARTS[c] * P, (STARTS[c] + SIZES[c]) * P)
 
-        def load_x(c):
-            nc.sync.dma_start(out=x_in[c][:], in_=x_bytes[0, rows_of(c), :].rearrange("(a p) k -> p a k", p=P))
+        def x_tile(c, a):
+            return x_first[:, a, :] if c == 0 else x_rest[:, STARTS[c] - SIZES[0] + a, :]
+
+        def load_x(dst, lo):
+            n = dst.shape[1] * P
+            nc.sync.dma_start(out=dst[:], in_=x_bytes[0, lo : lo + n, :].rearrange("(a p) k -> p a k", p=P))
 
         def load_words(w, src):
             nc.sync.dma_start(out=w_raw[w][:].bitcast(I32), in_=src[0].bitcast(I32))
@@ -84,20 +90,18 @@ def tile_selfattention_pa_w4_kernel(tc, x_bytes, x_scale, wp_words, wp_scales, b
         nc.vector.memset(s_raw[1][:].bitcast(I32), 0)
         nc.vector.memset(s_raw[0][:].bitcast(I32), 0)
         nc.vector.memset(bias_rows[:], 0.0)
-        load_x(0)
+        load_x(x_first, 0)
         load_scales(1, wt_scales)
-        load_x(1)
+        load_x(x_rest, SIZES[0] * P)
         load_words(1, wt_words)
-        load_scales(0, wp_scales)
-        load_words(0, wp_words)
-        load_x(2)
-        load_x(3)
-        make_identity(nc, ident_bf[:])
         for w, b in enumerate((b_phi, b_theta)):
-            nc.gpsimd.dma_start(
+            nc.sync.dma_start(
                 out=bias_rows[T * w : T * (w + 1), :].rearrange("t (b i) -> t b i", b=16),
                 in_=b.rearrange("(b t i) -> t b i", b=16, t=T),
             )
+        load_scales(0, wp_scales)
+        load_words(0, wp_words)
+        make_identity(nc, ident_bf[:])
         nc.vector.tensor_copy(out=ident[:], in_=ident_bf[:])
 
         bank, tile_of = {}, {}
@@ -123,25 +127,25 @@ def tile_selfattention_pa_w4_kernel(tc, x_bytes, x_scale, wp_words, wp_scales, b
             nc.vector.tensor_copy(out=bias[:], in_=bank["bias"][:, 0 : 2 * T])
 
         def cast(c):
-            xw = per_chunk.tile([P, A, FEATURES], BF16, name="xw")
+            xw = keep.tile([P, SIZES[c], FEATURES], BF16, name=f"xw{c}")
             tile_of["xw", c] = xw
-            for a in range(A):
+            for a in range(SIZES[c]):
                 if c in (0,):
-                    nc.vector.tensor_copy(out=xw[:, a, :], in_=x_in[c][:, a, :].bitcast(E4M3))
+                    nc.vector.tensor_copy(out=xw[:, a, :], in_=x_tile(c, a).bitcast(E4M3))
                 else:
-                    nc.scalar.copy(out=xw[:, a, :], in_=x_in[c][:, a, :].bitcast(E4M3))
+                    nc.scalar.copy(out=xw[:, a, :], in_=x_tile(c, a).bitcast(E4M3))
 
         def turn(c):
-            for a in range(A):
+            for a in range(SIZES[c]):
                 bk = psum.tile([P, T, P], BF16, name="bank")
                 bank["turn", c, a] = bk
                 for t in range(T):
                     nc.tensor.transpose(bk[:, t, :], tile_of["xw", c][:, a, t:FEATURES:T], ident_bf[:])
 
         def xm(c):
-            xg = per_chunk.tile([P, W, T], BF16, name="xg", align_bytes=64)
+            xg = keep.tile([P, SIZES[c] * P, T], BF16, name=f"xg{c}", align_bytes=64)
             tile_of["xg", c] = xg
-            for a in range(A):
+            for a in range(SIZES[c]):
                 nc.vector.tensor_tensor(
                     out=xg[:, a * P : (a + 1) * P, :],
                     in0=bank["turn", c, a][:].rearrange("p t r -> p r t"),
@@ -150,8 +154,8 @@ def tile_selfattention_pa_w4_kernel(tc, x_bytes, x_scale, wp_words, wp_scales, b
                 )
 
         def qx(c):
-            xq = per_chunk.tile([P, W], U32, name="xq", align_bytes=64)
-            xs = per_chunk.tile([P, W], U8, name="xs", align_bytes=64)
+            xq = keep.tile([P, SIZES[c] * P], U32, name=f"xq{c}", align_bytes=64)
+            xs = keep.tile([P, SIZES[c] * P], U8, name=f"xs{c}", align_bytes=64)
             tile_of["xq", c], tile_of["xs", c] = xq, xs
             nc.vector.quantize_mx(out=xq[:].bitcast(E4M3X4), scales=xs[:], in_=tile_of["xg", c][:].rearrange("p n t -> p (n t)"))
 
@@ -167,23 +171,25 @@ def tile_selfattention_pa_w4_kernel(tc, x_bytes, x_scale, wp_words, wp_scales, b
             )
 
         def first_tile(w, c):
-            for a in range(A):
+            for a in range(SIZES[c]):
                 bk = psum.tile([P, T, P], F32, name="bank")
                 bank["tile", w, c, a] = bk
                 for t in range(T):
                     mx_first(bk[:, t, :], w, t, c, slice(a * P, (a + 1) * P))
 
         def first_wide(w, c):
-            for h in range(2):
-                bk = psum.tile([P, 2, W], F32, name="bank")
+            n = SIZES[c]
+            k = T // n
+            for h in range(n):
+                bk = psum.tile([P, k, n * P], F32, name="bank")
                 bank["wide", w, c, h] = bk
-                for e in range(2):
-                    mx_first(bk[:, e, :], w, 2 * h + e, c, slice(0, W))
+                for e in range(k):
+                    mx_first(bk[:, e, :], w, k * h + e, c, slice(0, n * P))
 
         def take_v(w, c):
-            g = per_chunk.tile([P, W, T], BF16, name=f"woven{w}", align_bytes=64)
+            g = keep.tile([P, SIZES[c] * P, T], BF16, name=f"woven{w}_{c}", align_bytes=64)
             tile_of["woven", w, c] = g
-            for a in range(A):
+            for a in range(SIZES[c]):
                 nc.vector.tensor_tensor(
                     out=g[:, a * P : (a + 1) * P, :],
                     in0=bank["tile", w, c, a][:].rearrange("p t r -> p r t"),
@@ -192,15 +198,16 @@ def tile_selfattention_pa_w4_kernel(tc, x_bytes, x_scale, wp_words, wp_scales, b
                 )
 
         def take_s(w, c):
-            g = per_chunk.tile([P, T, W], BF16, name=f"rows{w}")
+            g = keep.tile([P, T, SIZES[c] * P], BF16, name=f"rows{w}_{c}")
             tile_of["rows", w, c] = g
+            k = T // SIZES[c]
             for t in range(T):
                 nc.scalar.activation(
-                    out=g[:, t, :], in_=bank["wide", w, c, t // 2][:, t % 2, :], func=ACT.Identity, bias=bias[:, T * w + t : T * w + t + 1], scale=1.0
+                    out=g[:, t, :], in_=bank["wide", w, c, t // k][:, t % k, :], func=ACT.Identity, bias=bias[:, T * w + t : T * w + t + 1], scale=1.0
                 )
 
         def weave(w, c):
-            g = per_chunk.tile([P, W, T], BF16, name=f"woven{w}", align_bytes=64)
+            g = keep.tile([P, SIZES[c] * P, T], BF16, name=f"woven{w}_{c}", align_bytes=64)
             tile_of["woven", w, c] = g
             src = tile_of["rows", w, c][:].rearrange("p t n -> p n t")
             if "g" == "g":
@@ -212,10 +219,10 @@ def tile_selfattention_pa_w4_kernel(tc, x_bytes, x_scale, wp_words, wp_scales, b
             nc.vector.quantize_mx(out=codes[w][:, rows_of(c)].bitcast(E4M3X4), scales=planes[w][:, rows_of(c)], in_=tile_of["woven", w, c][:].rearrange("p n t -> p (n t)"))
 
         def second(w, a, b):
-            bk = psum.tile([P, A, W], F32, name="bank")
+            bk = psum.tile([P, SIZES[a], SIZES[b] * P], F32, name="bank")
             bank["ab"[w], a, b] = bk
-            for i in range(A):
-                rows = slice((A * a + i) * P, (A * a + i + 1) * P)
+            for i in range(SIZES[a]):
+                rows = slice((STARTS[a] + i) * P, (STARTS[a] + i + 1) * P)
                 nc.tensor.matmul_mx(
                     out=bk[:, i, :],
                     lhsT=codes[w][:, rows].bitcast(E4M3X4),
@@ -227,22 +234,22 @@ def tile_selfattention_pa_w4_kernel(tc, x_bytes, x_scale, wp_words, wp_scales, b
                 )
 
         def u(a, b):
-            t = results.tile([P, A, W], F32, name="u")
+            t = keep.tile([P, SIZES[a], SIZES[b] * P], F32, name=f"u{a}_{b}")
             tile_of["u", a, b] = t
             nc.scalar.activation(out=t[:], in_=bank["a", a, b][:], func=ACT.Relu)
 
         def r(a, b):
-            t = results.tile([P, A, W], F32, name="r")
+            t = keep.tile([P, SIZES[a], SIZES[b] * P], F32, name=f"r{a}_{b}")
             tile_of["r", a, b] = t
             nc.scalar.activation(out=t[:], in_=bank["a", a, b][:], func=ACT.Relu, scale=HALF_SCALE)
 
         def stt(a, b):
-            t = results.tile([P, A, W], F32, name="o")
+            t = keep.tile([P, SIZES[a], SIZES[b] * P], F32, name=f"o{a}_{b}")
             tile_of["o", a, b] = t
             nc.vector.scalar_tensor_tensor(out=t[:], in0=bank["b", a, b][:], scalar=0.0, in1=tile_of["u", a, b][:], op0=ALU.max, op1=ALU.add)
 
         def d(a, b):
-            t = results.tile([P, A, W], F32, name="d")
+            t = keep.tile([P, SIZES[a], SIZES[b] * P], F32, name=f"d{a}_{b}")
             tile_of["d", a, b] = t
             mode = {}.get((a, b), "g")
             if mode == "g":
@@ -253,10 +260,10 @@ def tile_selfattention_pa_w4_kernel(tc, x_bytes, x_scale, wp_words, wp_scales, b
                 nc.vector.tensor_scalar(out=t[:], in0=tile_of["o", a, b][:], scalar1=HALF_SCALE, scalar2=None, op0=ALU.mult)
 
         def mirror(kind, name, a, b):
-            bk = psum.tile([P, A, A, P], F32, name="bank")
+            bk = psum.tile([P, SIZES[b], SIZES[a], P], F32, name="bank")
             bank[name, a, b] = bk
-            for j in range(A):
-                for i in range(A):
+            for j in range(SIZES[b]):
+                for i in range(SIZES[a]):
                     nc.tensor.transpose(bk[:, j, i, :], tile_of[kind, a, b][:, i, j * P : (j + 1) * P], ident[:])
 
         def mT(a, b):
@@ -266,12 +273,12 @@ def tile_selfattention_pa_w4_kernel(tc, x_bytes, x_scale, wp_words, wp_scales, b
             mirror("r", "rt", a, b)
 
         def e(a, b):
-            t = results.tile([P, A, W], F32, name="e")
+            t = keep.tile([P, SIZES[b], SIZES[a] * P], F32, name=f"e{a}_{b}")
             tile_of["e", a, b] = t
             nc.scalar.activation(out=t[:].rearrange("p j q -> p (j q)"), in_=bank["m", a, b][:].rearrange("p j i q -> p (j i q)"), func=ACT.Copy, scale=HALF_SCALE)
 
         def add(a, b):
-            t = results.tile([P, A, W], F32, name="s")
+            t = keep.tile([P, SIZES[a], SIZES[b] * P], F32, name=f"s{a}_{b}")
             tile_of["s", a, b] = t
             nc.vector.tensor_tensor(
                 out=t[:].rearrange("p i q -> p (i q)"), in0=bank["rt", a, b][:].rearrange("p j i q -> p (j i q)"), in1=tile_of["r", a, b][:].rearrange("p i q -> p (i q)"), op=ALU.add

from contextlib import ExitStack
import math

import concourse.mybir as mybir
from concourse.masks import make_identity

TOKENS, FEATURES, HIDDEN = 1024, 512, 512
FLOPS = 2 * 2 * TOKENS * FEATURES * HIDDEN + 2 * TOKENS * TOKENS * HIDDEN
HALF_SCALE = 0.5 / math.sqrt(512.0)

F32 = mybir.dt.float32
BF16 = mybir.dt.bfloat16
U8 = mybir.dt.uint8
U32 = mybir.dt.uint32
I32 = mybir.dt.int32
E4M3 = mybir.dt.float8_e4m3fn
E4M3X4 = mybir.dt.float8_e4m3fn_x4
E2M1X4 = mybir.dt.float4_e2m1fn_x4
ALU = mybir.AluOpType
ACT = mybir.ActivationFunctionType

P = 128
T = 4
SIZES = (2, 2, 2, 1, 1)
STARTS = [sum(SIZES[:c]) for c in range(len(SIZES))]
N_CH = len(SIZES)
ORDER = """
cast:1 cast:0 turn:0 xm:0 ps:1 pw:1 qx:0 cast:3 cast:2 turn:1
xm:1 bT bias pw:0 wide:1:0 takes:1:0 ps:0 turn:2 qx:1 tile:0:1
xm:2 takev:0:1 wide:1:1 takes:1:1 cast:4 tile:0:0 turn:3 weave:1:0 qx:2 wide:1:2
takes:1:2 takev:0:0 tile:0:2 turn:4 xm:3 weave:1:1 quant:0:0 quant:1:1 second:0:0:1 u:0:1
quant:1:0 second:0:0:0 r:0:0 quant:0:1 second:1:0:1 qx:3 wide:1:3 takes:1:3 second:0:1:1 r:1:1
tile:0:3 takev:0:2 rT:0:0 weave:1:2 stt:0:1 mT:0:1 e:0:1 quant:1:2 second:0:0:2 second:0:1:2
u:1:2 quant:0:2 second:1:1:2 second:0:2:2 r:2:2 xm:4 d:0:1 weave:1:3 store_d:0:1 store_e:0:1
u:0:2 rT:1:1 takev:0:3 second:1:0:2 add:0:0 qx:4 wide:1:4 store_s:0:0 quant:0:3 second:1:0:3
quant:1:3 second:0:0:3 takes:1:4 stt:1:2 d:1:2 add:1:1 store_s:1:1 second:0:1:3 u:1:3 rT:2:2
store_d:1:2 u:0:3 stt:0:2 add:2:2 store_s:2:2 mT:1:2 second:1:1:3 stt:1:3 e:1:2 store_e:1:2
stt:0:3 mT:0:2 e:0:2 weave:1:4 quant:1:4 tile:0:4 takev:0:4 store_e:0:2 second:0:3:3 r:3:3
mT:1:3 e:1:3 store_e:1:3 d:1:3 store_d:1:3 second:0:2:3 u:2:3 second:0:3:4 d:0:3 store_d:0:3
second:0:1:4 quant:0:4 second:0:0:4 u:3:4 second:1:2:3 stt:2:3 u:0:4 d:0:2 store_d:0:2 d:2:3
second:0:2:4 u:2:4 store_d:2:3 mT:0:3 e:0:3 store_e:0:3 second:1:3:4 stt:3:4 u:1:4 second:1:2:4
stt:2:4 second:0:4:4 r:4:4 second:1:0:4 d:3:4 store_d:3:4 mT:2:3 e:2:3 store_e:2:3 second:1:1:4
stt:0:4 d:2:4 store_d:2:4 mT:3:4 e:3:4 store_e:3:4 stt:1:4 rT:4:4 add:4:4 store_s:4:4
rT:3:3 d:0:4 add:3:3 store_s:3:3 store_d:0:4 d:1:4 store_d:1:4 mT:1:4 e:1:4 store_e:1:4
mT:0:4 e:0:4 store_e:0:4 mT:2:4 e:2:4 store_e:2:4
"""


def tile_selfattention_pa_w4_kernel(tc, x_bytes, x_scale, wp_words, wp_scales, b_phi, wt_words, wt_scales, b_theta, out):
    nc = tc.nc
    with ExitStack() as ctx:
        keep = ctx.enter_context(tc.tile_pool(name="keep", bufs=1))
        psum = ctx.enter_context(tc.psum_pool(name="psum", bufs=8))
        ctx.enter_context(tc.manual_schedule())

        w_raw, s_raw, w_perm, s_perm, codes, planes = [], [], [], [], [], []
        for w in range(2):
            w_raw.append(keep.tile([P, 2 * HIDDEN], U8, name=f"w_raw{w}", align_bytes=64))
            s_raw.append(keep.tile([P, HIDDEN], U8, name=f"s_raw{w}", align_bytes=64))
            w_perm.append(keep.tile([P, 2 * HIDDEN], U8, name=f"w_perm{w}", align_bytes=64))
            s_perm.append(keep.tile([P, HIDDEN], U8, name=f"s_perm{w}", align_bytes=64))
            codes.append(keep.tile([P, TOKENS], U32, name=f"codes{w}", align_bytes=64))
            planes.append(keep.tile([P, TOKENS], U8, name=f"planes{w}", align_bytes=64))
        x_first = keep.tile([P, SIZES[0], FEATURES], U8, name="x_first")
        x_rest = keep.tile([P, TOKENS // P - SIZES[0], FEATURES], U8, name="x_rest")
        k_scale = keep.tile([P, T], F32, name="k_scale")
        bias_rows = keep.tile([P, P], BF16, name="bias_rows")
        bias = keep.tile([P, 2 * T], F32, name="bias")
        ident_bf = keep.tile([P, P], BF16, name="ident_bf")
        ident = keep.tile([P, P], F32, name="ident")

        def rows_of(c):
            return slice(STARTS[c] * P, (STARTS[c] + SIZES[c]) * P)

        def x_tile(c, a):
            return x_first[:, a, :] if c == 0 else x_rest[:, STARTS[c] - SIZES[0] + a, :]

        def load_x(dst, lo):
            n = dst.shape[1] * P
            nc.sync.dma_start(out=dst[:], in_=x_bytes[0, lo : lo + n, :].rearrange("(a p) k -> p a k", p=P))

        def load_words(w, src):
            nc.sync.dma_start(out=w_raw[w][:].bitcast(I32), in_=src[0].bitcast(I32))

        def load_scales(w, src):
            for q in range(4):
                nc.sync.dma_start(out=s_raw[w][32 * q : 32 * q + 4, :].bitcast(I32), in_=src[0, 4 * q : 4 * q + 4, :].bitcast(I32))

        nc.scalar.dma_start(out=k_scale[:], in_=x_scale.rearrange("o q (p t) -> p (o q t)", t=T))
        nc.vector.memset(s_raw[1][:].bitcast(I32), 0)
        nc.vector.memset(s_raw[0][:].bitcast(I32), 0)
        nc.vector.memset(bias_rows[:], 0.0)
        load_x(x_first, 0)
        load_scales(1, wt_scales)
        load_x(x_rest, SIZES[0] * P)
        load_words(1, wt_words)
        for w, b in enumerate((b_phi, b_theta)):
            nc.sync.dma_start(
                out=bias_rows[T * w : T * (w + 1), :].rearrange("t (b i) -> t b i", b=16),
                in_=b.rearrange("(b t i) -> t b i", b=16, t=T),
            )
        load_scales(0, wp_scales)
        load_words(0, wp_words)
        make_identity(nc, ident_bf[:])
        nc.vector.tensor_copy(out=ident[:], in_=ident_bf[:])

        bank, tile_of = {}, {}

        def permute(dst, src):
            nc.vector.tensor_copy(
                out=dst[:].bitcast(I32).rearrange("p (t b c) -> p t b c", t=T, b=16),
                in_=src[:].bitcast(I32).rearrange("p (b t c) -> p t b c", t=T, b=16),
            )

        def pw(w):
            permute(w_perm[w], w_raw[w])

        def ps(w):
            permute(s_perm[w], s_raw[w])

        def bias_turn():
            bk = psum.tile([P, P], BF16, name="bank")
            bank["bias"] = bk
            nc.tensor.transpose(bk[:], bias_rows[:], ident_bf[:])

        def bias_take():
            nc.vector.tensor_copy(out=bias[:], in_=bank["bias"][:, 0 : 2 * T])

        def cast(c):
            xw = keep.tile([P, SIZES[c], FEATURES], BF16, name=f"xw{c}")
            tile_of["xw", c] = xw
            for a in range(SIZES[c]):
                if c in (0,):
                    nc.vector.tensor_copy(out=xw[:, a, :], in_=x_tile(c, a).bitcast(E4M3))
                else:
                    nc.scalar.copy(out=xw[:, a, :], in_=x_tile(c, a).bitcast(E4M3))

        def turn(c):
            for a in range(SIZES[c]):
                bk = psum.tile([P, T, P], BF16, name="bank")
                bank["turn", c, a] = bk
                for t in range(T):
                    nc.tensor.transpose(bk[:, t, :], tile_of["xw", c][:, a, t:FEATURES:T], ident_bf[:])

        def xm(c):
            xg = keep.tile([P, SIZES[c] * P, T], BF16, name=f"xg{c}", align_bytes=64)
            tile_of["xg", c] = xg
            for a in range(SIZES[c]):
                nc.vector.tensor_tensor(
                    out=xg[:, a * P : (a + 1) * P, :],
                    in0=bank["turn", c, a][:].rearrange("p t r -> p r t"),
                    in1=k_scale[:].unsqueeze(1).to_broadcast([P, P, T]),
                    op=ALU.mult,
                )

        def qx(c):
            xq = keep.tile([P, SIZES[c] * P], U32, name=f"xq{c}", align_bytes=64)
            xs = keep.tile([P, SIZES[c] * P], U8, name=f"xs{c}", align_bytes=64)
            tile_of["xq", c], tile_of["xs", c] = xq, xs
            nc.vector.quantize_mx(out=xq[:].bitcast(E4M3X4), scales=xs[:], in_=tile_of["xg", c][:].rearrange("p n t -> p (n t)"))

        def mx_first(dst, w, t, c, cols):
            nc.tensor.matmul_mx(
                out=dst,
                lhsT=w_perm[w][:, 2 * P * t : 2 * P * (t + 1)].bitcast(E2M1X4),
                lhsT_scale=s_perm[w][:, P * t : P * (t + 1)],
                rhs=tile_of["xq", c][:, cols].bitcast(E4M3X4),
                rhs_scale=tile_of["xs", c][:, cols],
                start=True,
                stop=True,
            )

        def first_tile(w, c):
            for a in range(SIZES[c]):
                bk = psum.tile([P, T, P], F32, name="bank")
                bank["tile", w, c, a] = bk
                for t in range(T):
                    mx_first(bk[:, t, :], w, t, c, slice(a * P, (a + 1) * P))

        def first_wide(w, c):
            n = SIZES[c]
            k = T // n
            for h in range(n):
                bk = psum.tile([P, k, n * P], F32, name="bank")
                bank["wide", w, c, h] = bk
                for e in range(k):
                    mx_first(bk[:, e, :], w, k * h + e, c, slice(0, n * P))

        def take_v(w, c):
            g = keep.tile([P, SIZES[c] * P, T], BF16, name=f"woven{w}_{c}", align_bytes=64)
            tile_of["woven", w, c] = g
            for a in range(SIZES[c]):
                nc.vector.tensor_tensor(
                    out=g[:, a * P : (a + 1) * P, :],
                    in0=bank["tile", w, c, a][:].rearrange("p t r -> p r t"),
                    in1=bias[:, T * w : T * (w + 1)].unsqueeze(1).to_broadcast([P, P, T]),
                    op=ALU.add,
                )

        def take_s(w, c):
            g = keep.tile([P, T, SIZES[c] * P], BF16, name=f"rows{w}_{c}")
            tile_of["rows", w, c] = g
            k = T // SIZES[c]
            for t in range(T):
                nc.scalar.activation(
                    out=g[:, t, :], in_=bank["wide", w, c, t // k][:, t % k, :], func=ACT.Identity, bias=bias[:, T * w + t : T * w + t + 1], scale=1.0
                )

        def weave(w, c):
            g = keep.tile([P, SIZES[c] * P, T], BF16, name=f"woven{w}_{c}", align_bytes=64)
            tile_of["woven", w, c] = g
            src = tile_of["rows", w, c][:].rearrange("p t n -> p n t")
            if "g" == "g":
                nc.gpsimd.tensor_scalar(out=g[:], in0=src, scalar1=1.0, scalar2=0.0, op0=ALU.mult, op1=ALU.add)
            else:
                nc.vector.tensor_copy(out=g[:], in_=src)

        def quant(w, c):
            nc.vector.quantize_mx(out=codes[w][:, rows_of(c)].bitcast(E4M3X4), scales=planes[w][:, rows_of(c)], in_=tile_of["woven", w, c][:].rearrange("p n t -> p (n t)"))

        def second(w, a, b):
            bk = psum.tile([P, SIZES[a], SIZES[b] * P], F32, name="bank")
            bank["ab"[w], a, b] = bk
            for i in range(SIZES[a]):
                rows = slice((STARTS[a] + i) * P, (STARTS[a] + i + 1) * P)
                nc.tensor.matmul_mx(
                    out=bk[:, i, :],
                    lhsT=codes[w][:, rows].bitcast(E4M3X4),
                    lhsT_scale=planes[w][:, rows],
                    rhs=codes[1 - w][:, rows_of(b)].bitcast(E4M3X4),
                    rhs_scale=planes[1 - w][:, rows_of(b)],
                    start=True,
                    stop=True,
                )

        def u(a, b):
            t = keep.tile([P, SIZES[a], SIZES[b] * P], F32, name=f"u{a}_{b}")
            tile_of["u", a, b] = t
            nc.scalar.activation(out=t[:], in_=bank["a", a, b][:], func=ACT.Relu)

        def r(a, b):
            t = keep.tile([P, SIZES[a], SIZES[b] * P], F32, name=f"r{a}_{b}")
            tile_of["r", a, b] = t
            nc.scalar.activation(out=t[:], in_=bank["a", a, b][:], func=ACT.Relu, scale=HALF_SCALE)

        def stt(a, b):
            t = keep.tile([P, SIZES[a], SIZES[b] * P], F32, name=f"o{a}_{b}")
            tile_of["o", a, b] = t
            nc.vector.scalar_tensor_tensor(out=t[:], in0=bank["b", a, b][:], scalar=0.0, in1=tile_of["u", a, b][:], op0=ALU.max, op1=ALU.add)

        def d(a, b):
            t = keep.tile([P, SIZES[a], SIZES[b] * P], F32, name=f"d{a}_{b}")
            tile_of["d", a, b] = t
            mode = {}.get((a, b), "g")
            if mode == "g":
                nc.gpsimd.tensor_scalar(out=t[:], in0=tile_of["o", a, b][:], scalar1=HALF_SCALE, scalar2=0.0, op0=ALU.mult, op1=ALU.add)
            elif mode == "s":
                nc.scalar.activation(out=t[:], in_=tile_of["o", a, b][:], func=ACT.Copy, scale=HALF_SCALE)
            else:
                nc.vector.tensor_scalar(out=t[:], in0=tile_of["o", a, b][:], scalar1=HALF_SCALE, scalar2=None, op0=ALU.mult)

        def mirror(kind, name, a, b):
            bk = psum.tile([P, SIZES[b], SIZES[a], P], F32, name="bank")
            bank[name, a, b] = bk
            for j in range(SIZES[b]):
                for i in range(SIZES[a]):
                    nc.tensor.transpose(bk[:, j, i, :], tile_of[kind, a, b][:, i, j * P : (j + 1) * P], ident[:])

        def mT(a, b):
            mirror("o", "m", a, b)

        def rT(a, b):
            mirror("r", "rt", a, b)

        def e(a, b):
            t = keep.tile([P, SIZES[b], SIZES[a] * P], F32, name=f"e{a}_{b}")
            tile_of["e", a, b] = t
            nc.scalar.activation(out=t[:].rearrange("p j q -> p (j q)"), in_=bank["m", a, b][:].rearrange("p j i q -> p (j i q)"), func=ACT.Copy, scale=HALF_SCALE)

        def add(a, b):
            t = keep.tile([P, SIZES[a], SIZES[b] * P], F32, name=f"s{a}_{b}")
            tile_of["s", a, b] = t
            nc.vector.tensor_tensor(
                out=t[:].rearrange("p i q -> p (i q)"), in0=bank["rt", a, b][:].rearrange("p j i q -> p (j i q)"), in1=tile_of["r", a, b][:].rearrange("p i q -> p (i q)"), op=ALU.add
            )

        def put(a, b, t):
            nc.sync.dma_start(out=out[0, rows_of(a), rows_of(b)].rearrange("(i p) q -> p i q", p=P), in_=t[:])

        def store_s(a, b):
            put(a, b, tile_of["s", a, b])

        def store_d(a, b):
            put(a, b, tile_of["d", a, b])

        def store_e(a, b):
            put(b, a, tile_of["e", a, b])

        stages = {
            "pw": pw, "ps": ps, "bT": bias_turn, "bias": bias_take, "cast": cast, "turn": turn, "xm": xm, "qx": qx,
            "tile": first_tile, "wide": first_wide, "takev": take_v, "takes": take_s, "weave": weave, "quant": quant,
            "second": second, "u": u, "r": r, "stt": stt, "d": d, "mT": mT, "rT": rT, "e": e, "add": add,
            "store_s": store_s, "store_d": store_d, "store_e": store_e,
        }
        for step in ORDER.split():
            parts = step.split(":")
            stages[parts[0]](*[int(v) for v in parts[1:]])
